import numpy as np
import ml_dtypes

BF16 = ml_dtypes.bfloat16


def bf(x):
    return np.asarray(x, np.float32).astype(BF16)


def f32(x):
    return np.asarray(x, np.float32)


def f64(x):
    return np.asarray(x).astype(np.float64)


def striped(idx):
    return np.tile(idx.reshape(-1, 16).T, (8, 1))


E, A, C, T, S, N = 8, 128, 512, 128, 2048, 1024


def sigmoid(v):
    return 1.0 / (1.0 + np.exp(-v))


def setup_inputs():
    return {"base": f32(np.random.standard_normal((C, S))), "actions": bf(np.random.standard_normal((A, N))), "w": bf(np.random.standard_normal((E, A, C)) / np.sqrt(A)), "b": f32(0.1 * np.random.standard_normal((C, E))), "offs": striped(np.random.permutation(S)[:N])}


def reference(base, actions, w, b, offs):
    idx = offs[:16].T.reshape(-1)
    xs = f64(actions).reshape(A, E, T)
    h = np.einsum("eac,aet->cet", f64(w), xs) + f64(b)[:, :, None]
    h = h.reshape(C, N)
    out = f64(base).copy()
    out[:, idx] = h * sigmoid(h)
    return out

@@ -1,0 +1,63 @@
+import concourse.mybir as mybir
+
+P = 128
+E = 8
+T = 128
+C = 512
+S = 2048
+N = E * T
+BLOCKS = C // P
+BANK = 512
+PER_BANK = BANK // T
+
+FLOPS = 2 * P * C * N
+
+BF16, F32, U16 = mybir.dt.bfloat16, mybir.dt.float32, mybir.dt.uint16
+MULT = mybir.AluOpType.mult
+IDENTITY = mybir.ActivationFunctionType.Identity
+SIGMOID = mybir.ActivationFunctionType.Sigmoid
+
+
+def tile_multiembodimentactionencoder_kernel(tc, base, actions, w, b, offs, out):
+    nc = tc.nc
+    with (
+        tc.tile_pool(name="held", bufs=1) as held,
+        tc.tile_pool(name="blocks", bufs=BLOCKS) as blocks,
+        tc.psum_pool(name="psum", bufs=BLOCKS * N // BANK) as psum,
+    ):
+        offsets = held.tile([P, N // 16], U16, name="offsets")
+        nc.sync.dma_start(offsets[:], offs)
+        tokens = held.tile([P, N], BF16, name="tokens")
+        nc.sync.dma_start(tokens[:], actions)
+        bias = held.tile([P, BLOCKS, E], F32, name="bias")
+        nc.sync.dma_start(bias[:], b.rearrange("(k p) e -> p k e", p=P))
+
+        windows, weights = [], []
+        for k in range(BLOCKS):
+            channels = slice(k * P, (k + 1) * P)
+            weight = blocks.tile([P, E, P], BF16, name="weight")
+            nc.sync.dma_start(weight[:], w[:, :, channels].rearrange("e a c -> a e c"))
+            window = blocks.tile([P, S], F32, name="window")
+            nc.sync.dma_start(window[:], base[channels, :])
+            weights.append(weight)
+            windows.append(window)
+
+        for k in range(BLOCKS):
+            h = blocks.tile([P, N], F32, name="h")
+            gate = blocks.tile([P, N], F32, name="gate")
+            for first in range(0, E, PER_BANK):
+                product = psum.tile([P, BANK], F32, name="product")
+                for e in range(first, first + PER_BANK):
+                    nc.tensor.matmul(
+                        product[:, (e - first) * T : (e - first + 1) * T],
+                        weights[k][:, e, :],
+                        tokens[:, e * T : (e + 1) * T],
+                        start=True,
+                        stop=True,
+                    )
+                for e in range(first, first + PER_BANK):
+                    in_bank = product[:, (e - first) * T : (e - first + 1) * T]
+                    nc.scalar.activation(h[:, e * T : (e + 1) * T], in_bank, IDENTITY, bias=bias[:, k, e : e + 1])
+                    nc.scalar.activation(gate[:, e * T : (e + 1) * T], in_bank, SIGMOID, bias=bias[:, k, e : e + 1])
+            nc.vector.tensor_tensor(windows[k][:].indirect(offsets[:]), h[:], gate[:], MULT)
+            nc.sync.dma_start(out[k * P : (k + 1) * P, :], windows[k][:])

@@ -28,18 +28,20 @@ def tile_multiembodimentactionencoder_kernel(tc, base, actions, w, b, offs, out)
         offsets = held.tile([P, N // 16], U16, name="offsets")
         nc.sync.dma_start(offsets[:], offs)
         tokens = held.tile([P, N], BF16, name="tokens")
-        nc.sync.dma_start(tokens[:], actions)
-        bias = held.tile([P, BLOCKS, E], F32, name="bias")
-        nc.sync.dma_start(bias[:], b.rearrange("(k p) e -> p k e", p=P))
+        nc.scalar.dma_start(tokens[:], actions)
 
-        windows, weights = [], []
+        windows, weights, biases = [], [], []
         for k in range(BLOCKS):
             channels = slice(k * P, (k + 1) * P)
+            queue = nc.scalar if k == 0 else nc.sync
             weight = blocks.tile([P, E, P], BF16, name="weight")
-            nc.sync.dma_start(weight[:], w[:, :, channels].rearrange("e a c -> a e c"))
+            queue.dma_start(weight[:], w[:, :, channels].rearrange("e a c -> a e c"))
+            bias = blocks.tile([P, E], F32, name="bias")
+            queue.dma_start(bias[:], b[channels, :])
             window = blocks.tile([P, S], F32, name="window")
             nc.sync.dma_start(window[:], base[channels, :])
             weights.append(weight)
+            biases.append(bias)
             windows.append(window)
 
         for k in range(BLOCKS):
@@ -57,7 +59,7 @@ def tile_multiembodimentactionencoder_kernel(tc, base, actions, w, b, offs, out)
                     )
                 for e in range(first, first + PER_BANK):
                     in_bank = product[:, (e - first) * T : (e - first + 1) * T]
-                    nc.scalar.activation(h[:, e * T : (e + 1) * T], in_bank, IDENTITY, bias=bias[:, k, e : e + 1])
-                    nc.scalar.activation(gate[:, e * T : (e + 1) * T], in_bank, SIGMOID, bias=bias[:, k, e : e + 1])
+                    nc.scalar.activation(h[:, e * T : (e + 1) * T], in_bank, IDENTITY, bias=biases[k][:, e : e + 1])
+                    nc.scalar.activation(gate[:, e * T : (e + 1) * T], in_bank, SIGMOID, bias=biases[k][:, e : e + 1])
             nc.vector.tensor_tensor(windows[k][:].indirect(offsets[:]), h[:], gate[:], MULT)
             nc.sync.dma_start(out[k * P : (k + 1) * P, :], windows[k][:])

@@ -23,21 +23,26 @@ def tile_multiembodimentactionencoder_kernel(tc, base, actions, w, b, offs, out)
     with (
         tc.tile_pool(name="held", bufs=1) as held,
         tc.tile_pool(name="blocks", bufs=BLOCKS) as blocks,
+        tc.tile_pool(name="pieces", bufs=BLOCKS * N // BANK) as pieces,
         tc.psum_pool(name="psum", bufs=BLOCKS * N // BANK) as psum,
     ):
-        offsets = held.tile([P, N // 16], U16, name="offsets")
-        nc.sync.dma_start(offsets[:], offs)
-        tokens = held.tile([P, N], BF16, name="tokens")
-        nc.scalar.dma_start(tokens[:], actions)
+        zeros = held.tile([P, 1], F32, name="zeros")
+        nc.gpsimd.memset(zeros[:], 0.0)
+        warmed = held.tile([P, 1], F32, name="warmed")
+        nc.scalar.activation(warmed[:], zeros[:], SIGMOID)
 
+        tokens = held.tile([P, N], BF16, name="tokens")
+        nc.sync.dma_start(tokens[:], actions)
+        offsets = held.tile([P, N // 16], U16, name="offsets")
         windows, weights, biases = [], [], []
         for k in range(BLOCKS):
             channels = slice(k * P, (k + 1) * P)
-            queue = nc.scalar if k == 0 else nc.sync
             weight = blocks.tile([P, E, P], BF16, name="weight")
-            queue.dma_start(weight[:], w[:, :, channels].rearrange("e a c -> a e c"))
+            nc.sync.dma_start(weight[:], w[:, :, channels].rearrange("e a c -> a e c"))
             bias = blocks.tile([P, E], F32, name="bias")
-            queue.dma_start(bias[:], b[channels, :])
+            nc.sync.dma_start(bias[:], b[channels, :])
+            if k == 0:
+                nc.sync.dma_start(offsets[:], offs)
             window = blocks.tile([P, S], F32, name="window")
             nc.sync.dma_start(window[:], base[channels, :])
             weights.append(weight)
@@ -45,21 +50,28 @@ def tile_multiembodimentactionencoder_kernel(tc, base, actions, w, b, offs, out)
             windows.append(window)
 
         for k in range(BLOCKS):
-            h = blocks.tile([P, N], F32, name="h")
-            gate = blocks.tile([P, N], F32, name="gate")
-            for first in range(0, E, PER_BANK):
+            for piece in range(N // BANK):
                 product = psum.tile([P, BANK], F32, name="product")
-                for e in range(first, first + PER_BANK):
+                h = pieces.tile([P, BANK], F32, name="h")
+                gate = pieces.tile([P, BANK], F32, name="gate")
+                for q in range(PER_BANK):
+                    e = piece * PER_BANK + q
                     nc.tensor.matmul(
-                        product[:, (e - first) * T : (e - first + 1) * T],
+                        product[:, q * T : (q + 1) * T],
                         weights[k][:, e, :],
                         tokens[:, e * T : (e + 1) * T],
                         start=True,
                         stop=True,
                     )
-                for e in range(first, first + PER_BANK):
-                    in_bank = product[:, (e - first) * T : (e - first + 1) * T]
-                    nc.scalar.activation(h[:, e * T : (e + 1) * T], in_bank, IDENTITY, bias=biases[k][:, e : e + 1])
-                    nc.scalar.activation(gate[:, e * T : (e + 1) * T], in_bank, SIGMOID, bias=biases[k][:, e : e + 1])
-            nc.vector.tensor_tensor(windows[k][:].indirect(offsets[:]), h[:], gate[:], MULT)
+                for q in range(PER_BANK):
+                    e = piece * PER_BANK + q
+                    cols = slice(q * T, (q + 1) * T)
+                    nc.scalar.activation(h[:, cols], product[:, cols], IDENTITY, bias=biases[k][:, e : e + 1])
+                    nc.scalar.activation(gate[:, cols], product[:, cols], SIGMOID, bias=biases[k][:, e : e + 1])
+                nc.vector.tensor_tensor(
+                    windows[k][:].indirect(offsets[:, piece * (BANK // 16) : (piece + 1) * (BANK // 16)]),
+                    h[:],
+                    gate[:],
+                    MULT,
+                )
             nc.sync.dma_start(out[k * P : (k + 1) * P, :], windows[k][:])

@@ -23,7 +23,6 @@ def tile_multiembodimentactionencoder_kernel(tc, base, actions, w, b, offs, out)
     with (
         tc.tile_pool(name="held", bufs=1) as held,
         tc.tile_pool(name="blocks", bufs=BLOCKS) as blocks,
-        tc.tile_pool(name="pieces", bufs=BLOCKS * N // BANK) as pieces,
         tc.psum_pool(name="psum", bufs=BLOCKS * N // BANK) as psum,
     ):
         zeros = held.tile([P, 1], F32, name="zeros")
@@ -50,28 +49,21 @@ def tile_multiembodimentactionencoder_kernel(tc, base, actions, w, b, offs, out)
             windows.append(window)
 
         for k in range(BLOCKS):
-            for piece in range(N // BANK):
+            h = blocks.tile([P, N], F32, name="h")
+            gate = blocks.tile([P, N], F32, name="gate")
+            for first in range(0, E, PER_BANK):
                 product = psum.tile([P, BANK], F32, name="product")
-                h = pieces.tile([P, BANK], F32, name="h")
-                gate = pieces.tile([P, BANK], F32, name="gate")
-                for q in range(PER_BANK):
-                    e = piece * PER_BANK + q
+                for e in range(first, first + PER_BANK):
                     nc.tensor.matmul(
-                        product[:, q * T : (q + 1) * T],
+                        product[:, (e - first) * T : (e - first + 1) * T],
                         weights[k][:, e, :],
                         tokens[:, e * T : (e + 1) * T],
                         start=True,
                         stop=True,
                     )
-                for q in range(PER_BANK):
-                    e = piece * PER_BANK + q
-                    cols = slice(q * T, (q + 1) * T)
-                    nc.scalar.activation(h[:, cols], product[:, cols], IDENTITY, bias=biases[k][:, e : e + 1])
-                    nc.scalar.activation(gate[:, cols], product[:, cols], SIGMOID, bias=biases[k][:, e : e + 1])
-                nc.vector.tensor_tensor(
-                    windows[k][:].indirect(offsets[:, piece * (BANK // 16) : (piece + 1) * (BANK // 16)]),
-                    h[:],
-                    gate[:],
-                    MULT,
-                )
+                for e in range(first, first + PER_BANK):
+                    in_bank = product[:, (e - first) * T : (e - first + 1) * T]
+                    nc.scalar.activation(h[:, e * T : (e + 1) * T], in_bank, IDENTITY, bias=biases[k][:, e : e + 1])
+                    nc.scalar.activation(gate[:, e * T : (e + 1) * T], in_bank, SIGMOID, bias=biases[k][:, e : e + 1])
+            nc.vector.tensor_tensor(windows[k][:].indirect(offsets[:]), h[:], gate[:], MULT)
             nc.sync.dma_start(out[k * P : (k + 1) * P, :], windows[k][:])

@@ -9,6 +9,7 @@ N = E * T
 BLOCKS = C // P
 BANK = 512
 PER_BANK = BANK // T
+PER_COLUMN = 16
 
 FLOPS = 2 * P * C * N
 
@@ -31,22 +32,37 @@ def tile_multiembodimentactionencoder_kernel(tc, base, actions, w, b, offs, out)
         nc.scalar.activation(warmed[:], zeros[:], SIGMOID)
 
         tokens = held.tile([P, N], BF16, name="tokens")
-        nc.sync.dma_start(tokens[:], actions)
-        offsets = held.tile([P, N // 16], U16, name="offsets")
-        windows, weights, biases = [], [], []
-        for k in range(BLOCKS):
-            channels = slice(k * P, (k + 1) * P)
-            weight = blocks.tile([P, E, P], BF16, name="weight")
-            nc.sync.dma_start(weight[:], w[:, :, channels].rearrange("e a c -> a e c"))
-            bias = blocks.tile([P, E], F32, name="bias")
-            nc.sync.dma_start(bias[:], b[channels, :])
-            if k == 0:
-                nc.sync.dma_start(offsets[:], offs)
-            window = blocks.tile([P, S], F32, name="window")
-            nc.sync.dma_start(window[:], base[channels, :])
-            weights.append(weight)
-            biases.append(bias)
-            windows.append(window)
+        offsets = held.tile([P, N // PER_COLUMN], U16, name="offsets")
+        weights = [held.tile([P, E, P], BF16, name=f"weights{k}") for k in range(BLOCKS)]
+        biases = [held.tile([P, E], F32, name=f"bias{k}") for k in range(BLOCKS)]
+        windows = [held.tile([P, S], F32, name=f"window{k}") for k in range(BLOCKS)]
+
+        def load_tokens(first, last):
+            nc.sync.dma_start(tokens[:, first * T : last * T], actions[:, first * T : last * T])
+
+        def load_weights(k, first, last):
+            nc.sync.dma_start(
+                weights[k][:, first:last, :],
+                w[first:last, :, k * P : (k + 1) * P].rearrange("e a c -> a e c"),
+            )
+
+        def load_bias(k):
+            nc.sync.dma_start(biases[k][:], b[k * P : (k + 1) * P, :])
+
+        def load_window(k):
+            nc.sync.dma_start(windows[k][:], base[k * P : (k + 1) * P, :])
+
+        load_tokens(0, PER_BANK)
+        load_weights(0, 0, PER_BANK)
+        load_bias(0)
+        nc.sync.dma_start(offsets[:], offs)
+        load_window(0)
+        load_tokens(PER_BANK, E)
+        load_weights(0, PER_BANK, E)
+        for k in range(1, BLOCKS):
+            load_weights(k, 0, E)
+            load_bias(k)
+            load_window(k)
 
         for k in range(BLOCKS):
             h = blocks.tile([P, N], F32, name="h")
@@ -65,5 +81,13 @@ def tile_multiembodimentactionencoder_kernel(tc, base, actions, w, b, offs, out)
                     in_bank = product[:, (e - first) * T : (e - first + 1) * T]
                     nc.scalar.activation(h[:, e * T : (e + 1) * T], in_bank, IDENTITY, bias=biases[k][:, e : e + 1])
                     nc.scalar.activation(gate[:, e * T : (e + 1) * T], in_bank, SIGMOID, bias=biases[k][:, e : e + 1])
-            nc.vector.tensor_tensor(windows[k][:].indirect(offsets[:]), h[:], gate[:], MULT)
+
+            cut = BANK if k == 0 else N
+            for lo in range(0, N, cut):
+                nc.vector.tensor_tensor(
+                    windows[k][:].indirect(offsets[:, lo // PER_COLUMN : (lo + cut) // PER_COLUMN]),
+                    h[:, lo : lo + cut],
+                    gate[:, lo : lo + cut],
+                    MULT,
+                )
             nc.sync.dma_start(out[k * P : (k + 1) * P, :], windows[k][:])

@@ -23,7 +23,6 @@ def tile_multiembodimentactionencoder_kernel(tc, base, actions, w, b, offs, out)
     nc = tc.nc
     with (
         tc.tile_pool(name="held", bufs=1) as held,
-        tc.tile_pool(name="blocks", bufs=BLOCKS) as blocks,
         tc.psum_pool(name="psum", bufs=BLOCKS * N // BANK) as psum,
     ):
         zeros = held.tile([P, 1], F32, name="zeros")
@@ -36,6 +35,8 @@ def tile_multiembodimentactionencoder_kernel(tc, base, actions, w, b, offs, out)
         weights = [held.tile([P, E, P], BF16, name=f"weights{k}") for k in range(BLOCKS)]
         biases = [held.tile([P, E], F32, name=f"bias{k}") for k in range(BLOCKS)]
         windows = [held.tile([P, S], F32, name=f"window{k}") for k in range(BLOCKS)]
+        hs = [held.tile([P, N], F32, name=f"h{k}") for k in range(BLOCKS)]
+        gates = [held.tile([P, N], F32, name=f"gate{k}") for k in range(BLOCKS)]
 
         def load_tokens(first, last):
             nc.sync.dma_start(tokens[:, first * T : last * T], actions[:, first * T : last * T])
@@ -52,42 +53,56 @@ def tile_multiembodimentactionencoder_kernel(tc, base, actions, w, b, offs, out)
         def load_window(k):
             nc.sync.dma_start(windows[k][:], base[k * P : (k + 1) * P, :])
 
+        def encode(k, first):
+            product = psum.tile([P, BANK], F32, name="product")
+            for e in range(first, first + PER_BANK):
+                nc.tensor.matmul(
+                    product[:, (e - first) * T : (e - first + 1) * T],
+                    weights[k][:, e, :],
+                    tokens[:, e * T : (e + 1) * T],
+                    start=True,
+                    stop=True,
+                )
+            for e in range(first, first + PER_BANK):
+                in_bank = product[:, (e - first) * T : (e - first + 1) * T]
+                nc.scalar.activation(hs[k][:, e * T : (e + 1) * T], in_bank, IDENTITY, bias=biases[k][:, e : e + 1])
+                nc.scalar.activation(gates[k][:, e * T : (e + 1) * T], in_bank, SIGMOID, bias=biases[k][:, e : e + 1])
+
+        def place(k, lo, hi):
+            nc.vector.tensor_tensor(
+                windows[k][:].indirect(offsets[:, lo // PER_COLUMN : hi // PER_COLUMN]),
+                hs[k][:, lo:hi],
+                gates[k][:, lo:hi],
+                MULT,
+            )
+
+        def store(k):
+            nc.sync.dma_start(out[k * P : (k + 1) * P, :], windows[k][:])
+
         load_tokens(0, PER_BANK)
         load_weights(0, 0, PER_BANK)
         load_bias(0)
         nc.sync.dma_start(offsets[:], offs)
         load_window(0)
+        load_weights(1, 0, PER_BANK)
+        load_bias(1)
+        load_window(1)
         load_tokens(PER_BANK, E)
         load_weights(0, PER_BANK, E)
-        for k in range(1, BLOCKS):
+        load_weights(1, PER_BANK, E)
+        for k in range(2, BLOCKS):
             load_weights(k, 0, E)
             load_bias(k)
             load_window(k)
 
-        for k in range(BLOCKS):
-            h = blocks.tile([P, N], F32, name="h")
-            gate = blocks.tile([P, N], F32, name="gate")
+        for first in range(0, E, PER_BANK):
+            for k in range(2):
+                encode(k, first)
+                place(k, first * T, (first + PER_BANK) * T)
+        store(0)
+        store(1)
+        for k in range(2, BLOCKS):
             for first in range(0, E, PER_BANK):
-                product = psum.tile([P, BANK], F32, name="product")
-                for e in range(first, first + PER_BANK):
-                    nc.tensor.matmul(
-                        product[:, (e - first) * T : (e - first + 1) * T],
-                        weights[k][:, e, :],
-                        tokens[:, e * T : (e + 1) * T],
-                        start=True,
-                        stop=True,
-                    )
-                for e in range(first, first + PER_BANK):
-                    in_bank = product[:, (e - first) * T : (e - first + 1) * T]
-                    nc.scalar.activation(h[:, e * T : (e + 1) * T], in_bank, IDENTITY, bias=biases[k][:, e : e + 1])
-                    nc.scalar.activation(gate[:, e * T : (e + 1) * T], in_bank, SIGMOID, bias=biases[k][:, e : e + 1])
-
-            cut = BANK if k == 0 else N
-            for lo in range(0, N, cut):
-                nc.vector.tensor_tensor(
-                    windows[k][:].indirect(offsets[:, lo // PER_COLUMN : (lo + cut) // PER_COLUMN]),
-                    h[:, lo : lo + cut],
-                    gate[:, lo : lo + cut],
-                    MULT,
-                )
-            nc.sync.dma_start(out[k * P : (k + 1) * P, :], windows[k][:])
+                encode(k, first)
+            place(k, 0, N)
+            store(k)

@@ -8,7 +8,8 @@ S = 2048
 N = E * T
 BLOCKS = C // P
 BANK = 512
-PER_BANK = BANK // T
+GROUPS = [(0, 3), (3, 4), (4, 8)]
+PAIR = 2
 PER_COLUMN = 16
 
 FLOPS = 2 * P * C * N
@@ -23,7 +24,7 @@ def tile_multiembodimentactionencoder_kernel(tc, base, actions, w, b, offs, out)
     nc = tc.nc
     with (
         tc.tile_pool(name="held", bufs=1) as held,
-        tc.psum_pool(name="psum", bufs=BLOCKS * N // BANK) as psum,
+        tc.psum_pool(name="psum", bufs=8) as psum,
     ):
         zeros = held.tile([P, 1], F32, name="zeros")
         nc.gpsimd.memset(zeros[:], 0.0)
@@ -32,7 +33,7 @@ def tile_multiembodimentactionencoder_kernel(tc, base, actions, w, b, offs, out)
 
         tokens = held.tile([P, N], BF16, name="tokens")
         offsets = held.tile([P, N // PER_COLUMN], U16, name="offsets")
-        weights = [held.tile([P, E, P], BF16, name=f"weights{k}") for k in range(BLOCKS)]
+        weights = [held.tile([P, E, PAIR * P], BF16, name=f"weights{k}") for k in range(BLOCKS // PAIR)]
         biases = [held.tile([P, E], F32, name=f"bias{k}") for k in range(BLOCKS)]
         windows = [held.tile([P, S], F32, name=f"window{k}") for k in range(BLOCKS)]
         hs = [held.tile([P, N], F32, name=f"h{k}") for k in range(BLOCKS)]
@@ -41,10 +42,10 @@ def tile_multiembodimentactionencoder_kernel(tc, base, actions, w, b, offs, out)
         def load_tokens(first, last):
             nc.sync.dma_start(tokens[:, first * T : last * T], actions[:, first * T : last * T])
 
-        def load_weights(k, first, last):
+        def load_weights(pair, first, last):
             nc.sync.dma_start(
-                weights[k][:, first:last, :],
-                w[first:last, :, k * P : (k + 1) * P].rearrange("e a c -> a e c"),
+                weights[pair][:, first:last, :],
+                w[first:last, :, pair * PAIR * P : (pair + 1) * PAIR * P].rearrange("e a c -> a e c"),
             )
 
         def load_bias(k):
@@ -53,22 +54,24 @@ def tile_multiembodimentactionencoder_kernel(tc, base, actions, w, b, offs, out)
         def load_window(k):
             nc.sync.dma_start(windows[k][:], base[k * P : (k + 1) * P, :])
 
-        def encode(k, first):
+        def encode(k, first, last):
             product = psum.tile([P, BANK], F32, name="product")
-            for e in range(first, first + PER_BANK):
+            column = (k % PAIR) * P
+            for e in range(first, last):
                 nc.tensor.matmul(
                     product[:, (e - first) * T : (e - first + 1) * T],
-                    weights[k][:, e, :],
+                    weights[k // PAIR][:, e, column : column + P],
                     tokens[:, e * T : (e + 1) * T],
                     start=True,
                     stop=True,
                 )
-            for e in range(first, first + PER_BANK):
+            for e in range(first, last):
                 in_bank = product[:, (e - first) * T : (e - first + 1) * T]
                 nc.scalar.activation(hs[k][:, e * T : (e + 1) * T], in_bank, IDENTITY, bias=biases[k][:, e : e + 1])
                 nc.scalar.activation(gates[k][:, e * T : (e + 1) * T], in_bank, SIGMOID, bias=biases[k][:, e : e + 1])
 
-        def place(k, lo, hi):
+        def place(k, first, last):
+            lo, hi = first * T, last * T
             nc.vector.tensor_tensor(
                 windows[k][:].indirect(offsets[:, lo // PER_COLUMN : hi // PER_COLUMN]),
                 hs[k][:, lo:hi],
@@ -79,30 +82,38 @@ def tile_multiembodimentactionencoder_kernel(tc, base, actions, w, b, offs, out)
         def store(k):
             nc.sync.dma_start(out[k * P : (k + 1) * P, :], windows[k][:])
 
-        load_tokens(0, PER_BANK)
-        load_weights(0, 0, PER_BANK)
+        load_tokens(0, 3)
+        load_weights(0, 0, 3)
         load_bias(0)
         nc.sync.dma_start(offsets[:], offs)
         load_window(0)
-        load_weights(1, 0, PER_BANK)
+        load_tokens(3, 4)
+        load_weights(0, 3, 4)
         load_bias(1)
         load_window(1)
-        load_tokens(PER_BANK, E)
-        load_weights(0, PER_BANK, E)
-        load_weights(1, PER_BANK, E)
-        for k in range(2, BLOCKS):
-            load_weights(k, 0, E)
+        for first in range(4, E, 2):
+            load_tokens(first, first + 2)
+            load_weights(0, first, first + 2)
+        for first, last in GROUPS:
+            load_weights(1, first, last)
+        for k in range(PAIR, BLOCKS):
             load_bias(k)
             load_window(k)
 
-        for first in range(0, E, PER_BANK):
-            for k in range(2):
-                encode(k, first)
-                place(k, first * T, (first + PER_BANK) * T)
+        encode(0, 0, 3)
+        place(0, 0, 3)
+        encode(1, 0, 3)
+        encode(1, 3, 4)
+        place(1, 0, 4)
+        encode(0, 3, 4)
+        encode(0, 4, E)
+        place(0, 3, E)
+        encode(1, 4, E)
+        place(1, 4, E)
         store(0)
         store(1)
         for k in range(2, BLOCKS):
-            for first in range(0, E, PER_BANK):
-                encode(k, first)
-            place(k, 0, N)
+            for first, last in GROUPS:
+                encode(k, first, last)
+            place(k, 0, E)
             store(k)

@@ -8,7 +8,7 @@ S = 2048
 N = E * T
 BLOCKS = C // P
 BANK = 512
-GROUPS = [(0, 3), (3, 4), (4, 8)]
+GROUPS = [(0, 3), (3, 6), (6, 8)]
 PAIR = 2
 PER_COLUMN = 16
 
@@ -87,31 +87,29 @@ def tile_multiembodimentactionencoder_kernel(tc, base, actions, w, b, offs, out)
         load_bias(0)
         nc.sync.dma_start(offsets[:], offs)
         load_window(0)
-        load_tokens(3, 4)
-        load_weights(0, 3, 4)
         load_bias(1)
         load_window(1)
-        for first in range(4, E, 2):
-            load_tokens(first, first + 2)
-            load_weights(0, first, first + 2)
+        for first, last in [(3, 4), (4, 6), (6, 8)]:
+            load_tokens(first, last)
+            load_weights(0, first, last)
         for first, last in GROUPS:
             load_weights(1, first, last)
         for k in range(PAIR, BLOCKS):
             load_bias(k)
             load_window(k)
 
-        encode(0, 0, 3)
-        place(0, 0, 3)
-        encode(1, 0, 3)
-        encode(1, 3, 4)
-        place(1, 0, 4)
-        encode(0, 3, 4)
-        encode(0, 4, E)
-        place(0, 3, E)
-        encode(1, 4, E)
-        place(1, 4, E)
-        store(0)
+        for k in range(2):
+            encode(k, 0, 3)
+            place(k, 0, 3)
+        encode(0, 3, 6)
+        place(0, 3, 6)
+        encode(1, 3, 6)
+        encode(1, 6, E)
+        place(1, 3, E)
+        encode(0, 6, E)
+        place(0, 6, E)
         store(1)
+        store(0)
         for k in range(2, BLOCKS):
             for first, last in GROUPS:
                 encode(k, first, last)

@@ -10,6 +10,7 @@ BLOCKS = C // P
 BANK = 512
 GROUPS = [(0, 3), (3, 6), (6, 8)]
 PAIR = 2
+ROW_ALIGN = 256
 PER_COLUMN = 16
 
 FLOPS = 2 * P * C * N
@@ -31,11 +32,13 @@ def tile_multiembodimentactionencoder_kernel(tc, base, actions, w, b, offs, out)
         warmed = held.tile([P, 1], F32, name="warmed")
         nc.scalar.activation(warmed[:], zeros[:], SIGMOID)
 
-        tokens = held.tile([P, N], BF16, name="tokens")
-        offsets = held.tile([P, N // PER_COLUMN], U16, name="offsets")
-        weights = [held.tile([P, E, PAIR * P], BF16, name=f"weights{k}") for k in range(BLOCKS // PAIR)]
-        biases = [held.tile([P, E], F32, name=f"bias{k}") for k in range(BLOCKS)]
-        windows = [held.tile([P, S], F32, name=f"window{k}") for k in range(BLOCKS)]
+        tokens = held.tile([P, N], BF16, name="tokens", align_bytes=ROW_ALIGN)
+        offsets = held.tile([P, N // PER_COLUMN], U16, name="offsets", align_bytes=ROW_ALIGN)
+        weights = [
+            held.tile([P, E, PAIR * P], BF16, name=f"weights{k}", align_bytes=ROW_ALIGN) for k in range(BLOCKS // PAIR)
+        ]
+        biases = [held.tile([P, E], F32, name=f"bias{k}", align_bytes=ROW_ALIGN) for k in range(BLOCKS)]
+        windows = [held.tile([P, S], F32, name=f"window{k}", align_bytes=ROW_ALIGN) for k in range(BLOCKS)]
         hs = [held.tile([P, N], F32, name=f"h{k}") for k in range(BLOCKS)]
         gates = [held.tile([P, N], F32, name=f"gate{k}") for k in range(BLOCKS)]
 

import concourse.mybir as mybir

P = 128
E = 8
T = 128
C = 512
S = 2048
N = E * T
BLOCKS = C // P
BANK = 512
GROUPS = [(0, 3), (3, 6), (6, 8)]
PAIR = 2
ROW_ALIGN = 256
PER_COLUMN = 16

FLOPS = 2 * P * C * N

BF16, F32, U16 = mybir.dt.bfloat16, mybir.dt.float32, mybir.dt.uint16
MULT = mybir.AluOpType.mult
IDENTITY = mybir.ActivationFunctionType.Identity
SIGMOID = mybir.ActivationFunctionType.Sigmoid


def tile_multiembodimentactionencoder_kernel(tc, base, actions, w, b, offs, out):
    nc = tc.nc
    with (
        tc.tile_pool(name="held", bufs=1) as held,
        tc.psum_pool(name="psum", bufs=8) as psum,
    ):
        zeros = held.tile([P, 1], F32, name="zeros")
        nc.gpsimd.memset(zeros[:], 0.0)
        warmed = held.tile([P, 1], F32, name="warmed")
        nc.scalar.activation(warmed[:], zeros[:], SIGMOID)

        tokens = held.tile([P, N], BF16, name="tokens", align_bytes=ROW_ALIGN)
        offsets = held.tile([P, N // PER_COLUMN], U16, name="offsets", align_bytes=ROW_ALIGN)
        weights = [
            held.tile([P, E, PAIR * P], BF16, name=f"weights{k}", align_bytes=ROW_ALIGN) for k in range(BLOCKS // PAIR)
        ]
        biases = [held.tile([P, E], F32, name=f"bias{k}", align_bytes=ROW_ALIGN) for k in range(BLOCKS)]
        windows = [held.tile([P, S], F32, name=f"window{k}", align_bytes=ROW_ALIGN) for k in range(BLOCKS)]
        hs = [held.tile([P, N], F32, name=f"h{k}") for k in range(BLOCKS)]
        gates = [held.tile([P, N], F32, name=f"gate{k}") for k in range(BLOCKS)]

        def load_tokens(first, last):
            nc.sync.dma_start(tokens[:, first * T : last * T], actions[:, first * T : last * T])

        def load_weights(pair, first, last):
            nc.sync.dma_start(
                weights[pair][:, first:last, :],
                w[first:last, :, pair * PAIR * P : (pair + 1) * PAIR * P].rearrange("e a c -> a e c"),
            )

        def load_bias(k):
            nc.sync.dma_start(biases[k][:], b[k * P : (k + 1) * P, :])

        def load_window(k):
            nc.sync.dma_start(windows[k][:], base[k * P : (k + 1) * P, :])

        def encode(k, first, last):
            product = psum.tile([P, BANK], F32, name="product")
            column = (k % PAIR) * P
            for e in range(first, last):
                nc.tensor.matmul(
                    product[:, (e - first) * T : (e - first + 1) * T],
                    weights[k // PAIR][:, e, column : column + P],
                    tokens[:, e * T : (e + 1) * T],
                    start=True,
                    stop=True,
                )
            for e in range(first, last):
                in_bank = product[:, (e - first) * T : (e - first + 1) * T]
                nc.scalar.activation(hs[k][:, e * T : (e + 1) * T], in_bank, IDENTITY, bias=biases[k][:, e : e + 1])
                nc.scalar.activation(gates[k][:, e * T : (e + 1) * T], in_bank, SIGMOID, bias=biases[k][:, e : e + 1])

        def place(k, first, last):
            lo, hi = first * T, last * T
            nc.vector.tensor_tensor(
                windows[k][:].indirect(offsets[:, lo // PER_COLUMN : hi // PER_COLUMN]),
                hs[k][:, lo:hi],
                gates[k][:, lo:hi],
                MULT,
            )

        def store(k):
            nc.sync.dma_start(out[k * P : (k + 1) * P, :], windows[k][:])

        load_tokens(0, 3)
        load_weights(0, 0, 3)
        load_bias(0)
        nc.sync.dma_start(offsets[:], offs)
        load_window(0)
        load_bias(1)
        load_window(1)
        for first, last in [(3, 4), (4, 6), (6, 8)]:
            load_tokens(first, last)
            load_weights(0, first, last)
        for first, last in GROUPS:
            load_weights(1, first, last)
        for k in range(PAIR, BLOCKS):
            load_bias(k)
            load_window(k)

        for k in range(2):
            encode(k, 0, 3)
            place(k, 0, 3)
        encode(0, 3, 6)
        place(0, 3, 6)
        encode(1, 3, 6)
        encode(1, 6, E)
        place(1, 3, E)
        encode(0, 6, E)
        place(0, 6, E)
        store(1)
        store(0)
        for k in range(2, BLOCKS):
            for first, last in GROUPS:
                encode(k, first, last)
            place(k, 0, E)
            store(k)
